import numpy as np
import ml_dtypes


def mxq(x, axis, fmt="e4m3"):
    dtype, down = {"e4m3": (ml_dtypes.float8_e4m3fn, 7), "e5m2": (ml_dtypes.float8_e5m2, 14)}[fmt]
    v = np.moveaxis(np.asarray(x, np.float32).astype(ml_dtypes.bfloat16).astype(np.float64), axis, -1)
    blocks = v.reshape(v.shape[:-1] + (-1, 32))
    amax = np.abs(blocks).max(-1, keepdims=True)
    byte = np.maximum(np.where(amax > 0, np.frexp(amax)[1] - 1 + 127, 0) - down, 1)
    scale = np.exp2(byte - 127.0)
    codes = (blocks / scale).astype(np.float32).astype(dtype).astype(np.float64)
    return np.moveaxis((codes * scale).reshape(v.shape), -1, axis)


WIDE = False


def mx_kscale(k):
    if not WIDE:
        return np.ones(k)
    levels = np.array([10, -10, 5, -5, 0])
    a = np.random.permutation(np.resize(levels, k // 512 * 4)).reshape(k // 512, 4)
    idx = np.arange(k)
    return np.exp2(a[idx // 512, idx % 128 // 32])


BF16 = ml_dtypes.bfloat16


def bf(x):
    return np.asarray(x, np.float32).astype(BF16)


def f64(x):
    return np.asarray(x).astype(np.float64)


E2M1 = np.array([0.0, 0.5, 1.0, 1.5, 2.0, 3.0, 4.0, 6.0, -0.0, -0.5, -1.0, -1.5, -2.0, -3.0, -4.0, -6.0])


def pack_weight(w, fmt):
    k, n = w.shape
    w = f64(bf(w)).reshape(k // 32, 32, n)
    amax = np.abs(w).max(1)
    if fmt == "e4m3":
        byte = np.frexp(amax)[1] - 1 + 127 - 7
    else:
        mant, ex = np.frexp(amax / 6.0)
        byte = np.where(mant > 0.5, ex, ex - 1) + 127
    byte = np.clip(np.where(amax > 0, byte, 1), 1, 254)
    scaled = (w * np.exp2(127.0 - byte)[:, None, :]).reshape(k, n).astype(np.float32)
    by_word = np.ascontiguousarray(scaled.reshape(k // 512, 128, 4, n).transpose(0, 1, 3, 2))
    if fmt == "e4m3":
        words = by_word.astype(ml_dtypes.float8_e4m3fn).view(np.uint8)
    else:
        c = by_word.astype(ml_dtypes.float4_e2m1fn).view(np.uint8) & 0xF
        words = c[..., 0::2] | (c[..., 1::2] << 4)
    return np.ascontiguousarray(words), np.ascontiguousarray(byte.astype(np.uint8).reshape(k // 512, 16, n))


def unpack_weight(words, scales, fmt):
    g, p, n, _ = words.shape
    if fmt == "e4m3":
        vals = np.ascontiguousarray(words).view(ml_dtypes.float8_e4m3fn).astype(np.float64)
    else:
        nib = np.empty((g, p, n, 4), np.uint8)
        nib[..., 0::2] = words & 0xF
        nib[..., 1::2] = words >> 4
        vals = E2M1[nib]
    vals = vals * np.repeat(np.exp2(scales.astype(np.float64) - 127.0), 8, axis=1)[..., None]
    return vals.transpose(0, 1, 3, 2).reshape(g * 512, n)

def pack4(w):
    words, scales = pack_weight(w, "e2m1")
    return words.reshape(words.shape[0], 128, -1), scales


def unpack4(words, scales):
    return unpack_weight(words.reshape(words.shape[0], 128, -1, 2), scales, "e2m1")


B, IN, MEM, CTX, H, G = 4096, 512, 512, 1024, 4, 3


def sigmoid(v):
    return 1.0 / (1.0 + np.exp(-v))


def setup_inputs():
    s = mx_kscale(IN)
    w = np.random.standard_normal((MEM, MEM + IN)) / np.sqrt(MEM + IN)
    w[:, MEM:] = w[:, MEM:] / s
    input_tensor = bf(np.random.standard_normal((B, IN)) * s)
    previous_memory = bf(np.random.standard_normal((B, MEM)))
    words, scales = pack4(np.ascontiguousarray(w.T))
    return {"input_tensor": input_tensor,
            "previous_memory": previous_memory,
            "fg_w_words": words,
            "fg_w_scales": scales,
            "fg_b": bf(np.random.standard_normal(MEM) * 0.3)}


def reference(input_tensor, previous_memory, fg_w_words, fg_w_scales, fg_b):
    m = f64(previous_memory)
    forget_in = np.concatenate([m, f64(input_tensor)], axis=-1)
    fgate = sigmoid((mxq(forget_in, 1, "e4m3") @ unpack4(fg_w_words, fg_w_scales)) + f64(fg_b))
    return m * fgate

@@ -1,0 +1,158 @@
+from contextlib import ExitStack
+
+import concourse.masks as masks
+import concourse.mybir as mybir
+
+F32 = mybir.dt.float32
+BF16 = mybir.dt.bfloat16
+I32 = mybir.dt.int32
+U32 = mybir.dt.uint32
+U8 = mybir.dt.uint8
+FP8X4 = mybir.dt.float8_e4m3fn_x4
+FP4X4 = mybir.dt.float4_e2m1fn_x4
+ADD = mybir.AluOpType.add
+MULT = mybir.AluOpType.mult
+SIGMOID = mybir.ActivationFunctionType.Sigmoid
+
+P = 128
+PACK = 4
+K_PASS = P * PACK
+WORDS = K_PASS // 2
+BATCH = 4096
+N_OUT = 512
+PASSES = 2
+ROW_TILES = BATCH // P
+TILES_PER_ROUND = 4
+ROUNDS = ROW_TILES // TILES_PER_ROUND
+VECTOR_TILES = TILES_PER_ROUND // 2
+PSUM_BANKS = 8
+
+FLOPS = 2 * BATCH * PASSES * K_PASS * N_OUT
+
+
+def tile_dynamicmemorycell_pa_t_kernel(
+    tc, input_tensor, previous_memory, fg_w_words, fg_w_scales, fg_b, out
+):
+    nc = tc.nc
+    mem_rows = previous_memory.rearrange("(p r) k -> p r k", r=ROW_TILES)
+    inp_rows = input_tensor.rearrange("(p r) k -> p r k", r=ROW_TILES)
+    out_rows = out.rearrange("(p r) n -> p r n", r=ROW_TILES)
+
+    with ExitStack() as ctx:
+        consts = ctx.enter_context(tc.tile_pool(name="consts", bufs=1))
+        resident = ctx.enter_context(tc.tile_pool(name="resident", bufs=ROUNDS))
+        work = ctx.enter_context(tc.tile_pool(name="work", bufs=3))
+        gates = ctx.enter_context(tc.tile_pool(name="gates", bufs=4))
+        transposed = ctx.enter_context(tc.psum_pool(name="transposed", bufs=PSUM_BANKS // 2))
+        sums = ctx.enter_context(tc.psum_pool(name="sums", bufs=PSUM_BANKS // 2))
+        ctx.enter_context(tc.manual_schedule())
+
+        w_scales = consts.tile([P, PASSES, N_OUT], U8, align_bytes=64)
+        nc.vector.memset(w_scales[:].rearrange("p g n -> p (g n)").bitcast(I32), 0)
+        warm = consts.tile([P, 1], F32)
+        nc.vector.memset(warm[:], 0.0)
+        nc.scalar.activation(out=warm[:], in_=warm[:], func=SIGMOID)
+        ident = consts.tile([P, P], F32)
+        masks.make_identity(nc, ident[:])
+
+        mem_tiles = []
+        inp_tiles = []
+
+        def load_round(c):
+            rows = slice(c * TILES_PER_ROUND, (c + 1) * TILES_PER_ROUND)
+            mem_sb = resident.tile([P, TILES_PER_ROUND, K_PASS], BF16)
+            nc.sync.dma_start(out=mem_sb[:], in_=mem_rows[:, rows, :])
+            mem_tiles.append(mem_sb)
+            inp_sb = resident.tile([P, TILES_PER_ROUND, K_PASS], BF16)
+            nc.sync.dma_start(out=inp_sb[:], in_=inp_rows[:, rows, :])
+            inp_tiles.append(inp_sb)
+
+        load_round(0)
+        scale_rows = fg_w_scales.bitcast(I32).rearrange("g q w -> q g w")
+        for quadrant in range(4):
+            nc.sync.dma_start(
+                out=w_scales[32 * quadrant : 32 * quadrant + 4, :, :].bitcast(I32),
+                in_=scale_rows[4 * quadrant : 4 * quadrant + 4, :, :],
+            )
+        w_words = consts.tile([P, PASSES, 2 * N_OUT], U8, align_bytes=64)
+        nc.sync.dma_start(
+            out=w_words[:].bitcast(I32), in_=fg_w_words.bitcast(I32).rearrange("g p w -> p g w")
+        )
+        bias = consts.tile([P, N_OUT], BF16)
+        nc.sync.dma_start(out=bias[:], in_=fg_b.partition_broadcast(P))
+        for c in range(1, ROUNDS):
+            load_round(c)
+
+        def transpose_round(c):
+            grouped = work.tile([P, TILES_PER_ROUND, PASSES, P, PACK], BF16, align_bytes=64)
+            for i in range(TILES_PER_ROUND):
+                planes = transposed.tile([P, PASSES * 2, P], F32)
+                for g, source in enumerate((mem_tiles[c], inp_tiles[c])):
+                    words = source[:, i, :].bitcast(F32)
+                    for u in range(2):
+                        nc.tensor.transpose(planes[:, 2 * g + u, :], words[:, u:WORDS:2], ident[:])
+                nc.scalar.copy(
+                    out=grouped[:, i, :, :, :]
+                    .rearrange("p g r t -> p (g r t)")
+                    .bitcast(F32)
+                    .rearrange("p (g r u) -> p g r u", g=PASSES, u=2),
+                    in_=planes[:].rearrange("p (g u) r -> p g r u", u=2),
+                )
+            return grouped
+
+        def quantise_round(grouped):
+            codes = work.tile([P, TILES_PER_ROUND, PASSES, P], U32, align_bytes=64)
+            scales = work.tile([P, TILES_PER_ROUND, PASSES, P], U8, align_bytes=64)
+            nc.vector.quantize_mx(
+                out=codes[:].rearrange("p i g r -> p (i g r)").bitcast(FP8X4),
+                scales=scales[:].rearrange("p i g r -> p (i g r)"),
+                in_=grouped[:].rearrange("p i g r t -> p (i g r t)"),
+            )
+            return codes, scales
+
+        def gate_round(codes, scales):
+            gate = gates.tile([P, TILES_PER_ROUND, N_OUT], F32)
+            for i in range(TILES_PER_ROUND):
+                acc = sums.tile([P, N_OUT], F32)
+                for g in range(PASSES):
+                    nc.tensor.matmul_mx(
+                        out=acc[:],
+                        lhsT=codes[:, i, g, :].bitcast(FP8X4),
+                        lhsT_scale=scales[:, i, g, :],
+                        rhs=w_words[:, g, :].bitcast(FP4X4),
+                        rhs_scale=w_scales[:, g, :],
+                        start=(g == 0),
+                        stop=(g == PASSES - 1),
+                    )
+                nc.vector.tensor_tensor(out=gate[:, i, :], in0=acc[:], in1=bias[:], op=ADD)
+            nc.scalar.activation(out=gate[:], in_=gate[:], func=SIGMOID)
+            return gate
+
+        def finish_round(c, gate):
+            mem_sb = mem_tiles[c]
+            nc.vector.tensor_tensor(
+                out=gate[:, :VECTOR_TILES, :],
+                in0=gate[:, :VECTOR_TILES, :],
+                in1=mem_sb[:, :VECTOR_TILES, :],
+                op=MULT,
+            )
+            nc.gpsimd.tensor_tensor(
+                out=gate[:, VECTOR_TILES:, :],
+                in0=gate[:, VECTOR_TILES:, :],
+                in1=mem_sb[:, VECTOR_TILES:, :],
+                op=MULT,
+            )
+            rows = slice(c * TILES_PER_ROUND, (c + 1) * TILES_PER_ROUND)
+            nc.sync.dma_start(out=out_rows[:, rows, :], in_=gate[:])
+
+        quantised = quantise_round(transpose_round(0))
+        gate_before = None
+        for c in range(ROUNDS):
+            grouped_next = transpose_round(c + 1) if c + 1 < ROUNDS else None
+            gate = gate_round(quantised[0], quantised[1])
+            if grouped_next is not None:
+                quantised = quantise_round(grouped_next)
+            if gate_before is not None:
+                finish_round(c - 1, gate_before)
+            gate_before = gate
+        finish_round(ROUNDS - 1, gate_before)

@@ -22,10 +22,13 @@ BATCH = 4096
 N_OUT = 512
 PASSES = 2
 ROW_TILES = BATCH // P
-TILES_PER_ROUND = 4
+TILES_PER_LOAD = 4
+LOADS = ROW_TILES // TILES_PER_LOAD
+TILES_PER_ROUND = 2
 ROUNDS = ROW_TILES // TILES_PER_ROUND
 VECTOR_TILES = TILES_PER_ROUND // 2
 PSUM_BANKS = 8
+RESULT_TILES = 16
 
 FLOPS = 2 * BATCH * PASSES * K_PASS * N_OUT
 
@@ -40,9 +43,9 @@ def tile_dynamicmemorycell_pa_t_kernel(
 
     with ExitStack() as ctx:
         consts = ctx.enter_context(tc.tile_pool(name="consts", bufs=1))
-        resident = ctx.enter_context(tc.tile_pool(name="resident", bufs=ROUNDS))
+        resident = ctx.enter_context(tc.tile_pool(name="resident", bufs=LOADS))
         work = ctx.enter_context(tc.tile_pool(name="work", bufs=3))
-        gates = ctx.enter_context(tc.tile_pool(name="gates", bufs=4))
+        gates = ctx.enter_context(tc.tile_pool(name="gates", bufs=RESULT_TILES // TILES_PER_ROUND))
         transposed = ctx.enter_context(tc.psum_pool(name="transposed", bufs=PSUM_BANKS // 2))
         sums = ctx.enter_context(tc.psum_pool(name="sums", bufs=PSUM_BANKS // 2))
         ctx.enter_context(tc.manual_schedule())
@@ -58,16 +61,21 @@ def tile_dynamicmemorycell_pa_t_kernel(
         mem_tiles = []
         inp_tiles = []
 
-        def load_round(c):
-            rows = slice(c * TILES_PER_ROUND, (c + 1) * TILES_PER_ROUND)
-            mem_sb = resident.tile([P, TILES_PER_ROUND, K_PASS], BF16)
+        def load_rows(j):
+            rows = slice(j * TILES_PER_LOAD, (j + 1) * TILES_PER_LOAD)
+            mem_sb = resident.tile([P, TILES_PER_LOAD, K_PASS], BF16)
             nc.sync.dma_start(out=mem_sb[:], in_=mem_rows[:, rows, :])
             mem_tiles.append(mem_sb)
-            inp_sb = resident.tile([P, TILES_PER_ROUND, K_PASS], BF16)
+            inp_sb = resident.tile([P, TILES_PER_LOAD, K_PASS], BF16)
             nc.sync.dma_start(out=inp_sb[:], in_=inp_rows[:, rows, :])
             inp_tiles.append(inp_sb)
 
-        load_round(0)
+        def round_of(tiles, c):
+            first = c * TILES_PER_ROUND
+            inside = first % TILES_PER_LOAD
+            return tiles[first // TILES_PER_LOAD][:, inside : inside + TILES_PER_ROUND, :]
+
+        load_rows(0)
         scale_rows = fg_w_scales.bitcast(I32).rearrange("g q w -> q g w")
         for quadrant in range(4):
             nc.sync.dma_start(
@@ -80,14 +88,14 @@ def tile_dynamicmemorycell_pa_t_kernel(
         )
         bias = consts.tile([P, N_OUT], BF16)
         nc.sync.dma_start(out=bias[:], in_=fg_b.partition_broadcast(P))
-        for c in range(1, ROUNDS):
-            load_round(c)
+        for j in range(1, LOADS):
+            load_rows(j)
 
         def transpose_round(c):
             grouped = work.tile([P, TILES_PER_ROUND, PASSES, P, PACK], BF16, align_bytes=64)
             for i in range(TILES_PER_ROUND):
                 planes = transposed.tile([P, PASSES * 2, P], F32)
-                for g, source in enumerate((mem_tiles[c], inp_tiles[c])):
+                for g, source in enumerate((round_of(mem_tiles, c), round_of(inp_tiles, c))):
                     words = source[:, i, :].bitcast(F32)
                     for u in range(2):
                         nc.tensor.transpose(planes[:, 2 * g + u, :], words[:, u:WORDS:2], ident[:])
@@ -129,7 +137,7 @@ def tile_dynamicmemorycell_pa_t_kernel(
             return gate
 
         def finish_round(c, gate):
-            mem_sb = mem_tiles[c]
+            mem_sb = round_of(mem_tiles, c)
             nc.vector.tensor_tensor(
                 out=gate[:, :VECTOR_TILES, :],
                 in0=gate[:, :VECTOR_TILES, :],

@@ -23,10 +23,8 @@ N_OUT = 512
 PASSES = 2
 ROW_TILES = BATCH // P
 TILES_PER_LOAD = 4
-LOADS = ROW_TILES // TILES_PER_LOAD
 TILES_PER_ROUND = 2
 ROUNDS = ROW_TILES // TILES_PER_ROUND
-VECTOR_TILES = TILES_PER_ROUND // 2
 PSUM_BANKS = 8
 RESULT_TILES = 16
 
@@ -41,9 +39,11 @@ def tile_dynamicmemorycell_pa_t_kernel(
     inp_rows = input_tensor.rearrange("(p r) k -> p r k", r=ROW_TILES)
     out_rows = out.rearrange("(p r) n -> p r n", r=ROW_TILES)
 
+    load_starts = list(range(TILES_PER_LOAD)) + list(range(TILES_PER_LOAD, ROW_TILES, TILES_PER_LOAD))
+
     with ExitStack() as ctx:
         consts = ctx.enter_context(tc.tile_pool(name="consts", bufs=1))
-        resident = ctx.enter_context(tc.tile_pool(name="resident", bufs=LOADS))
+        resident = ctx.enter_context(tc.tile_pool(name="resident", bufs=2 * len(load_starts)))
         work = ctx.enter_context(tc.tile_pool(name="work", bufs=3))
         gates = ctx.enter_context(tc.tile_pool(name="gates", bufs=RESULT_TILES // TILES_PER_ROUND))
         transposed = ctx.enter_context(tc.psum_pool(name="transposed", bufs=PSUM_BANKS // 2))
@@ -61,42 +61,36 @@ def tile_dynamicmemorycell_pa_t_kernel(
         mem_tiles = []
         inp_tiles = []
 
-        def load_rows(j):
-            rows = slice(j * TILES_PER_LOAD, (j + 1) * TILES_PER_LOAD)
-            mem_sb = resident.tile([P, TILES_PER_LOAD, K_PASS], BF16)
-            nc.sync.dma_start(out=mem_sb[:], in_=mem_rows[:, rows, :])
-            mem_tiles.append(mem_sb)
-            inp_sb = resident.tile([P, TILES_PER_LOAD, K_PASS], BF16)
-            nc.sync.dma_start(out=inp_sb[:], in_=inp_rows[:, rows, :])
-            inp_tiles.append(inp_sb)
+        def load_tiles(first, count):
+            for rows, tiles in ((mem_rows, mem_tiles), (inp_rows, inp_tiles)):
+                loaded = resident.tile([P, count, K_PASS], BF16)
+                nc.sync.dma_start(out=loaded[:], in_=rows[:, first : first + count, :])
+                tiles.extend([loaded[:, i, :] for i in range(count)])
 
-        def round_of(tiles, c):
-            first = c * TILES_PER_ROUND
-            inside = first % TILES_PER_LOAD
-            return tiles[first // TILES_PER_LOAD][:, inside : inside + TILES_PER_ROUND, :]
-
-        load_rows(0)
+        for first in load_starts[:TILES_PER_LOAD]:
+            load_tiles(first, 1)
+        w_words = consts.tile([P, PASSES, 2 * N_OUT], U8, align_bytes=64)
+        nc.sync.dma_start(
+            out=w_words[:].bitcast(I32), in_=fg_w_words.bitcast(I32).rearrange("g p w -> p g w")
+        )
         scale_rows = fg_w_scales.bitcast(I32).rearrange("g q w -> q g w")
         for quadrant in range(4):
             nc.sync.dma_start(
                 out=w_scales[32 * quadrant : 32 * quadrant + 4, :, :].bitcast(I32),
                 in_=scale_rows[4 * quadrant : 4 * quadrant + 4, :, :],
             )
-        w_words = consts.tile([P, PASSES, 2 * N_OUT], U8, align_bytes=64)
-        nc.sync.dma_start(
-            out=w_words[:].bitcast(I32), in_=fg_w_words.bitcast(I32).rearrange("g p w -> p g w")
-        )
         bias = consts.tile([P, N_OUT], BF16)
         nc.sync.dma_start(out=bias[:], in_=fg_b.partition_broadcast(P))
-        for j in range(1, LOADS):
-            load_rows(j)
+        for first in load_starts[TILES_PER_LOAD:]:
+            load_tiles(first, TILES_PER_LOAD)
 
-        def transpose_round(c):
+        def quantise_round(c):
             grouped = work.tile([P, TILES_PER_ROUND, PASSES, P, PACK], BF16, align_bytes=64)
             for i in range(TILES_PER_ROUND):
+                j = c * TILES_PER_ROUND + i
                 planes = transposed.tile([P, PASSES * 2, P], F32)
-                for g, source in enumerate((round_of(mem_tiles, c), round_of(inp_tiles, c))):
-                    words = source[:, i, :].bitcast(F32)
+                for g, source in enumerate((mem_tiles[j], inp_tiles[j])):
+                    words = source.bitcast(F32)
                     for u in range(2):
                         nc.tensor.transpose(planes[:, 2 * g + u, :], words[:, u:WORDS:2], ident[:])
                 nc.scalar.copy(
@@ -106,9 +100,6 @@ def tile_dynamicmemorycell_pa_t_kernel(
                     .rearrange("p (g r u) -> p g r u", g=PASSES, u=2),
                     in_=planes[:].rearrange("p (g u) r -> p g r u", u=2),
                 )
-            return grouped
-
-        def quantise_round(grouped):
             codes = work.tile([P, TILES_PER_ROUND, PASSES, P], U32, align_bytes=64)
             scales = work.tile([P, TILES_PER_ROUND, PASSES, P], U8, align_bytes=64)
             nc.vector.quantize_mx(
@@ -118,7 +109,7 @@ def tile_dynamicmemorycell_pa_t_kernel(
             )
             return codes, scales
 
-        def gate_round(codes, scales):
+        def multiply_round(codes, scales):
             gate = gates.tile([P, TILES_PER_ROUND, N_OUT], F32)
             for i in range(TILES_PER_ROUND):
                 acc = sums.tile([P, N_OUT], F32)
@@ -133,34 +124,28 @@ def tile_dynamicmemorycell_pa_t_kernel(
                         stop=(g == PASSES - 1),
                     )
                 nc.vector.tensor_tensor(out=gate[:, i, :], in0=acc[:], in1=bias[:], op=ADD)
-            nc.scalar.activation(out=gate[:], in_=gate[:], func=SIGMOID)
             return gate
 
         def finish_round(c, gate):
-            mem_sb = round_of(mem_tiles, c)
-            nc.vector.tensor_tensor(
-                out=gate[:, :VECTOR_TILES, :],
-                in0=gate[:, :VECTOR_TILES, :],
-                in1=mem_sb[:, :VECTOR_TILES, :],
-                op=MULT,
-            )
-            nc.gpsimd.tensor_tensor(
-                out=gate[:, VECTOR_TILES:, :],
-                in0=gate[:, VECTOR_TILES:, :],
-                in1=mem_sb[:, VECTOR_TILES:, :],
-                op=MULT,
-            )
+            for i in range(TILES_PER_ROUND):
+                nc.scalar.activation(out=gate[:, i, :], in_=gate[:, i, :], func=SIGMOID)
+            for i in range(TILES_PER_ROUND):
+                engine = nc.gpsimd if i % 2 == 0 else nc.vector
+                engine.tensor_tensor(
+                    out=gate[:, i, :],
+                    in0=gate[:, i, :],
+                    in1=mem_tiles[c * TILES_PER_ROUND + i],
+                    op=MULT,
+                )
             rows = slice(c * TILES_PER_ROUND, (c + 1) * TILES_PER_ROUND)
             nc.sync.dma_start(out=out_rows[:, rows, :], in_=gate[:])
 
-        quantised = quantise_round(transpose_round(0))
-        gate_before = None
-        for c in range(ROUNDS):
-            grouped_next = transpose_round(c + 1) if c + 1 < ROUNDS else None
-            gate = gate_round(quantised[0], quantised[1])
-            if grouped_next is not None:
-                quantised = quantise_round(grouped_next)
-            if gate_before is not None:
-                finish_round(c - 1, gate_before)
-            gate_before = gate
-        finish_round(ROUNDS - 1, gate_before)
+        quantised = {}
+        gate_of = {}
+        for n in range(-1, ROUNDS + 1):
+            if n + 1 < ROUNDS:
+                quantised[n + 1] = quantise_round(n + 1)
+            if 0 <= n < ROUNDS:
+                gate_of[n] = multiply_round(quantised[n][0], quantised[n][1])
+            if n >= 1:
+                finish_round(n - 1, gate_of[n - 1])

@@ -27,6 +27,8 @@ TILES_PER_ROUND = 2
 ROUNDS = ROW_TILES // TILES_PER_ROUND
 PSUM_BANKS = 8
 RESULT_TILES = 16
+IDLE_MATMULS_AT_START = 6
+IDLE_MATMULS_IN_STEP = 2
 
 FLOPS = 2 * BATCH * PASSES * K_PASS * N_OUT
 
@@ -50,6 +52,15 @@ def tile_dynamicmemorycell_pa_t_kernel(
         sums = ctx.enter_context(tc.psum_pool(name="sums", bufs=PSUM_BANKS // 2))
         ctx.enter_context(tc.manual_schedule())
 
+        zeros = consts.tile([P, N_OUT], BF16)
+        nc.vector.memset(zeros[:], 0.0)
+
+        def idle_matmuls(count):
+            unread = sums.tile([P, N_OUT], F32, tag="acc")
+            for k in range(count):
+                nc.tensor.matmul(out=unread[:], lhsT=zeros[:, :P], rhs=zeros[:], start=True, stop=True)
+
+        idle_matmuls(IDLE_MATMULS_AT_START)
         w_scales = consts.tile([P, PASSES, N_OUT], U8, align_bytes=64)
         nc.vector.memset(w_scales[:].rearrange("p g n -> p (g n)").bitcast(I32), 0)
         warm = consts.tile([P, 1], F32)
@@ -145,7 +156,9 @@ def tile_dynamicmemorycell_pa_t_kernel(
         for n in range(-1, ROUNDS + 1):
             if n + 1 < ROUNDS:
                 quantised[n + 1] = quantise_round(n + 1)
-            if 0 <= n < ROUNDS:
+            if n < 0:
+                idle_matmuls(IDLE_MATMULS_IN_STEP)
+            elif n < ROUNDS:
                 gate_of[n] = multiply_round(quantised[n][0], quantised[n][1])
             if n >= 1:
                 finish_round(n - 1, gate_of[n - 1])

@@ -27,8 +27,6 @@ TILES_PER_ROUND = 2
 ROUNDS = ROW_TILES // TILES_PER_ROUND
 PSUM_BANKS = 8
 RESULT_TILES = 16
-IDLE_MATMULS_AT_START = 6
-IDLE_MATMULS_IN_STEP = 2
 
 FLOPS = 2 * BATCH * PASSES * K_PASS * N_OUT
 
@@ -41,26 +39,29 @@ def tile_dynamicmemorycell_pa_t_kernel(
     inp_rows = input_tensor.rearrange("(p r) k -> p r k", r=ROW_TILES)
     out_rows = out.rearrange("(p r) n -> p r n", r=ROW_TILES)
 
-    load_starts = list(range(TILES_PER_LOAD)) + list(range(TILES_PER_LOAD, ROW_TILES, TILES_PER_LOAD))
+    head_starts = list(range(0, TILES_PER_LOAD, TILES_PER_ROUND))
+    body_starts = list(range(TILES_PER_LOAD, ROW_TILES, TILES_PER_LOAD))
 
     with ExitStack() as ctx:
         consts = ctx.enter_context(tc.tile_pool(name="consts", bufs=1))
-        resident = ctx.enter_context(tc.tile_pool(name="resident", bufs=2 * len(load_starts)))
+        resident = ctx.enter_context(tc.tile_pool(name="resident", bufs=2 * len(head_starts + body_starts)))
         work = ctx.enter_context(tc.tile_pool(name="work", bufs=3))
         gates = ctx.enter_context(tc.tile_pool(name="gates", bufs=RESULT_TILES // TILES_PER_ROUND))
         transposed = ctx.enter_context(tc.psum_pool(name="transposed", bufs=PSUM_BANKS // 2))
         sums = ctx.enter_context(tc.psum_pool(name="sums", bufs=PSUM_BANKS // 2))
         ctx.enter_context(tc.manual_schedule())
 
-        zeros = consts.tile([P, N_OUT], BF16)
-        nc.vector.memset(zeros[:], 0.0)
+        bias_row = consts.tile([P, N_OUT], BF16)
+        nc.vector.memset(bias_row[:], 0.0)
+        ones = consts.tile([P, P], BF16)
+        nc.vector.memset(ones[:], 1.0)
+        bias = consts.tile([P, N_OUT], F32)
 
-        def idle_matmuls(count):
-            unread = sums.tile([P, N_OUT], F32, tag="acc")
-            for k in range(count):
-                nc.tensor.matmul(out=unread[:], lhsT=zeros[:, :P], rhs=zeros[:], start=True, stop=True)
+        def spread_bias():
+            bias_sum = sums.tile([P, N_OUT], F32, tag="acc")
+            nc.tensor.matmul(out=bias_sum[:], lhsT=ones[:], rhs=bias_row[:], start=True, stop=True)
+            nc.vector.tensor_copy(out=bias[:], in_=bias_sum[:])
 
-        idle_matmuls(IDLE_MATMULS_AT_START)
         w_scales = consts.tile([P, PASSES, N_OUT], U8, align_bytes=64)
         nc.vector.memset(w_scales[:].rearrange("p g n -> p (g n)").bitcast(I32), 0)
         warm = consts.tile([P, 1], F32)
@@ -78,21 +79,21 @@ def tile_dynamicmemorycell_pa_t_kernel(
                 nc.sync.dma_start(out=loaded[:], in_=rows[:, first : first + count, :])
                 tiles.extend([loaded[:, i, :] for i in range(count)])
 
-        for first in load_starts[:TILES_PER_LOAD]:
-            load_tiles(first, 1)
-        w_words = consts.tile([P, PASSES, 2 * N_OUT], U8, align_bytes=64)
-        nc.sync.dma_start(
-            out=w_words[:].bitcast(I32), in_=fg_w_words.bitcast(I32).rearrange("g p w -> p g w")
-        )
+        load_tiles(head_starts[0], TILES_PER_ROUND)
+        nc.sync.dma_start(out=bias_row[0:1, :], in_=fg_b.unsqueeze(0))
         scale_rows = fg_w_scales.bitcast(I32).rearrange("g q w -> q g w")
         for quadrant in range(4):
             nc.sync.dma_start(
                 out=w_scales[32 * quadrant : 32 * quadrant + 4, :, :].bitcast(I32),
                 in_=scale_rows[4 * quadrant : 4 * quadrant + 4, :, :],
             )
-        bias = consts.tile([P, N_OUT], BF16)
-        nc.sync.dma_start(out=bias[:], in_=fg_b.partition_broadcast(P))
-        for first in load_starts[TILES_PER_LOAD:]:
+        w_words = consts.tile([P, PASSES, 2 * N_OUT], U8, align_bytes=64)
+        nc.sync.dma_start(
+            out=w_words[:].bitcast(I32), in_=fg_w_words.bitcast(I32).rearrange("g p w -> p g w")
+        )
+        for first in head_starts[1:]:
+            load_tiles(first, TILES_PER_ROUND)
+        for first in body_starts:
             load_tiles(first, TILES_PER_LOAD)
 
         def quantise_round(c):
@@ -148,8 +149,10 @@ def tile_dynamicmemorycell_pa_t_kernel(
                     in1=mem_tiles[c * TILES_PER_ROUND + i],
                     op=MULT,
                 )
-            rows = slice(c * TILES_PER_ROUND, (c + 1) * TILES_PER_ROUND)
-            nc.sync.dma_start(out=out_rows[:, rows, :], in_=gate[:])
+            count = TILES_PER_ROUND if c + 1 < ROUNDS else 1
+            for i in range(0, TILES_PER_ROUND, count):
+                first = c * TILES_PER_ROUND + i
+                nc.sync.dma_start(out=out_rows[:, first : first + count, :], in_=gate[:, i : i + count, :])
 
         quantised = {}
         gate_of = {}
@@ -157,7 +160,7 @@ def tile_dynamicmemorycell_pa_t_kernel(
             if n + 1 < ROUNDS:
                 quantised[n + 1] = quantise_round(n + 1)
             if n < 0:
-                idle_matmuls(IDLE_MATMULS_IN_STEP)
+                spread_bias()
             elif n < ROUNDS:
                 gate_of[n] = multiply_round(quantised[n][0], quantised[n][1])
             if n >= 1:

@@ -25,6 +25,7 @@ ROW_TILES = BATCH // P
 TILES_PER_LOAD = 4
 TILES_PER_ROUND = 2
 ROUNDS = ROW_TILES // TILES_PER_ROUND
+ROUNDS_AHEAD = 2
 PSUM_BANKS = 8
 RESULT_TILES = 16
 
@@ -156,12 +157,12 @@ def tile_dynamicmemorycell_pa_t_kernel(
 
         quantised = {}
         gate_of = {}
-        for n in range(-1, ROUNDS + 1):
-            if n + 1 < ROUNDS:
-                quantised[n + 1] = quantise_round(n + 1)
-            if n < 0:
+        for n in range(-ROUNDS_AHEAD, ROUNDS + 1):
+            if n + ROUNDS_AHEAD < ROUNDS:
+                quantised[n + ROUNDS_AHEAD] = quantise_round(n + ROUNDS_AHEAD)
+            if n == -1:
                 spread_bias()
-            elif n < ROUNDS:
+            elif 0 <= n < ROUNDS:
                 gate_of[n] = multiply_round(quantised[n][0], quantised[n][1])
             if n >= 1:
                 finish_round(n - 1, gate_of[n - 1])

@@ -23,9 +23,10 @@ N_OUT = 512
 PASSES = 2
 ROW_TILES = BATCH // P
 TILES_PER_LOAD = 4
+HEAD_TILES = 8
 TILES_PER_ROUND = 2
+ROUNDS_BEFORE_PASSES = 2
 ROUNDS = ROW_TILES // TILES_PER_ROUND
-ROUNDS_AHEAD = 2
 PSUM_BANKS = 8
 RESULT_TILES = 16
 
@@ -40,8 +41,8 @@ def tile_dynamicmemorycell_pa_t_kernel(
     inp_rows = input_tensor.rearrange("(p r) k -> p r k", r=ROW_TILES)
     out_rows = out.rearrange("(p r) n -> p r n", r=ROW_TILES)
 
-    head_starts = list(range(0, TILES_PER_LOAD, TILES_PER_ROUND))
-    body_starts = list(range(TILES_PER_LOAD, ROW_TILES, TILES_PER_LOAD))
+    head_starts = list(range(0, HEAD_TILES, TILES_PER_ROUND))
+    body_starts = list(range(HEAD_TILES, ROW_TILES, TILES_PER_LOAD))
 
     with ExitStack() as ctx:
         consts = ctx.enter_context(tc.tile_pool(name="consts", bufs=1))
@@ -80,7 +81,8 @@ def tile_dynamicmemorycell_pa_t_kernel(
                 nc.sync.dma_start(out=loaded[:], in_=rows[:, first : first + count, :])
                 tiles.extend([loaded[:, i, :] for i in range(count)])
 
-        load_tiles(head_starts[0], TILES_PER_ROUND)
+        for first in head_starts[:ROUNDS_BEFORE_PASSES]:
+            load_tiles(first, TILES_PER_ROUND)
         nc.sync.dma_start(out=bias_row[0:1, :], in_=fg_b.unsqueeze(0))
         scale_rows = fg_w_scales.bitcast(I32).rearrange("g q w -> q g w")
         for quadrant in range(4):
@@ -92,7 +94,7 @@ def tile_dynamicmemorycell_pa_t_kernel(
         nc.sync.dma_start(
             out=w_words[:].bitcast(I32), in_=fg_w_words.bitcast(I32).rearrange("g p w -> p g w")
         )
-        for first in head_starts[1:]:
+        for first in head_starts[ROUNDS_BEFORE_PASSES:]:
             load_tiles(first, TILES_PER_ROUND)
         for first in body_starts:
             load_tiles(first, TILES_PER_LOAD)
@@ -157,12 +159,12 @@ def tile_dynamicmemorycell_pa_t_kernel(
 
         quantised = {}
         gate_of = {}
-        for n in range(-ROUNDS_AHEAD, ROUNDS + 1):
-            if n + ROUNDS_AHEAD < ROUNDS:
-                quantised[n + ROUNDS_AHEAD] = quantise_round(n + ROUNDS_AHEAD)
-            if n == -1:
+        for n in range(-1, ROUNDS + 1):
+            if n + 1 < ROUNDS:
+                quantised[n + 1] = quantise_round(n + 1)
+            if n < 0:
                 spread_bias()
-            elif 0 <= n < ROUNDS:
+            elif n < ROUNDS:
                 gate_of[n] = multiply_round(quantised[n][0], quantised[n][1])
             if n >= 1:
                 finish_round(n - 1, gate_of[n - 1])

@@ -145,7 +145,7 @@ def tile_dynamicmemorycell_pa_t_kernel(
             for i in range(TILES_PER_ROUND):
                 nc.scalar.activation(out=gate[:, i, :], in_=gate[:, i, :], func=SIGMOID)
             for i in range(TILES_PER_ROUND):
-                engine = nc.gpsimd if i % 2 == 0 else nc.vector
+                engine = nc.gpsimd if i % 2 == 0 and c + 1 < ROUNDS else nc.vector
                 engine.tensor_tensor(
                     out=gate[:, i, :],
                     in0=gate[:, i, :],

@@ -29,6 +29,7 @@ ROUNDS_BEFORE_PASSES = 2
 ROUNDS = ROW_TILES // TILES_PER_ROUND
 PSUM_BANKS = 8
 RESULT_TILES = 16
+GPSIMD_COLUMNS = 464
 
 FLOPS = 2 * BATCH * PASSES * K_PASS * N_OUT
 
@@ -72,14 +73,19 @@ def tile_dynamicmemorycell_pa_t_kernel(
         ident = consts.tile([P, P], F32)
         masks.make_identity(nc, ident[:])
 
-        mem_tiles = []
-        inp_tiles = []
+        mem_rounds = []
+        inp_rounds = []
 
         def load_tiles(first, count):
-            for rows, tiles in ((mem_rows, mem_tiles), (inp_rows, inp_tiles)):
+            for rows, rounds in ((mem_rows, mem_rounds), (inp_rows, inp_rounds)):
                 loaded = resident.tile([P, count, K_PASS], BF16)
                 nc.sync.dma_start(out=loaded[:], in_=rows[:, first : first + count, :])
-                tiles.extend([loaded[:, i, :] for i in range(count)])
+                rounds.extend(
+                    [
+                        loaded[:, i : i + TILES_PER_ROUND, :].rearrange("p i k -> p (i k)")
+                        for i in range(0, count, TILES_PER_ROUND)
+                    ]
+                )
 
         for first in head_starts[:ROUNDS_BEFORE_PASSES]:
             load_tiles(first, TILES_PER_ROUND)
@@ -102,10 +108,9 @@ def tile_dynamicmemorycell_pa_t_kernel(
         def quantise_round(c):
             grouped = work.tile([P, TILES_PER_ROUND, PASSES, P, PACK], BF16, align_bytes=64)
             for i in range(TILES_PER_ROUND):
-                j = c * TILES_PER_ROUND + i
                 planes = transposed.tile([P, PASSES * 2, P], F32)
-                for g, source in enumerate((mem_tiles[j], inp_tiles[j])):
-                    words = source.bitcast(F32)
+                for g, source in enumerate((mem_rounds[c], inp_rounds[c])):
+                    words = source[:, i * K_PASS : (i + 1) * K_PASS].bitcast(F32)
                     for u in range(2):
                         nc.tensor.transpose(planes[:, 2 * g + u, :], words[:, u:WORDS:2], ident[:])
                 nc.scalar.copy(
@@ -144,13 +149,17 @@ def tile_dynamicmemorycell_pa_t_kernel(
         def finish_round(c, gate):
             for i in range(TILES_PER_ROUND):
                 nc.scalar.activation(out=gate[:, i, :], in_=gate[:, i, :], func=SIGMOID)
-            for i in range(TILES_PER_ROUND):
-                engine = nc.gpsimd if i % 2 == 0 and c + 1 < ROUNDS else nc.vector
+            flat = gate[:].rearrange("p i n -> p (i n)")
+            if c + 1 < ROUNDS:
+                shares = (
+                    (nc.gpsimd, slice(0, GPSIMD_COLUMNS)),
+                    (nc.vector, slice(GPSIMD_COLUMNS, TILES_PER_ROUND * N_OUT)),
+                )
+            else:
+                shares = tuple((nc.vector, slice(i * N_OUT, (i + 1) * N_OUT)) for i in range(TILES_PER_ROUND))
+            for engine, columns in shares:
                 engine.tensor_tensor(
-                    out=gate[:, i, :],
-                    in0=gate[:, i, :],
-                    in1=mem_tiles[c * TILES_PER_ROUND + i],
-                    op=MULT,
+                    out=flat[:, columns], in0=flat[:, columns], in1=mem_rounds[c][:, columns], op=MULT
                 )
             count = TILES_PER_ROUND if c + 1 < ROUNDS else 1
             for i in range(0, TILES_PER_ROUND, count):

@@ -65,7 +65,7 @@ def tile_dynamicmemorycell_pa_t_kernel(
             nc.tensor.matmul(out=bias_sum[:], lhsT=ones[:], rhs=bias_row[:], start=True, stop=True)
             nc.vector.tensor_copy(out=bias[:], in_=bias_sum[:])
 
-        w_scales = consts.tile([P, PASSES, N_OUT], U8, align_bytes=64)
+        w_scales = consts.tile([P, PASSES, N_OUT], U8, align_bytes=256)
         nc.vector.memset(w_scales[:].rearrange("p g n -> p (g n)").bitcast(I32), 0)
         warm = consts.tile([P, 1], F32)
         nc.vector.memset(warm[:], 0.0)
@@ -96,7 +96,7 @@ def tile_dynamicmemorycell_pa_t_kernel(
                 out=w_scales[32 * quadrant : 32 * quadrant + 4, :, :].bitcast(I32),
                 in_=scale_rows[4 * quadrant : 4 * quadrant + 4, :, :],
             )
-        w_words = consts.tile([P, PASSES, 2 * N_OUT], U8, align_bytes=64)
+        w_words = consts.tile([P, PASSES, 2 * N_OUT], U8, align_bytes=256)
         nc.sync.dma_start(
             out=w_words[:].bitcast(I32), in_=fg_w_words.bitcast(I32).rearrange("g p w -> p g w")
         )
@@ -106,7 +106,7 @@ def tile_dynamicmemorycell_pa_t_kernel(
             load_tiles(first, TILES_PER_LOAD)
 
         def quantise_round(c):
-            grouped = work.tile([P, TILES_PER_ROUND, PASSES, P, PACK], BF16, align_bytes=64)
+            grouped = work.tile([P, TILES_PER_ROUND, PASSES, P, PACK], BF16, align_bytes=256)
             for i in range(TILES_PER_ROUND):
                 planes = transposed.tile([P, PASSES * 2, P], F32)
                 for g, source in enumerate((mem_rounds[c], inp_rounds[c])):
@@ -120,8 +120,8 @@ def tile_dynamicmemorycell_pa_t_kernel(
                     .rearrange("p (g r u) -> p g r u", g=PASSES, u=2),
                     in_=planes[:].rearrange("p (g u) r -> p g r u", u=2),
                 )
-            codes = work.tile([P, TILES_PER_ROUND, PASSES, P], U32, align_bytes=64)
-            scales = work.tile([P, TILES_PER_ROUND, PASSES, P], U8, align_bytes=64)
+            codes = work.tile([P, TILES_PER_ROUND, PASSES, P], U32, align_bytes=256)
+            scales = work.tile([P, TILES_PER_ROUND, PASSES, P], U8, align_bytes=256)
             nc.vector.quantize_mx(
                 out=codes[:].rearrange("p i g r -> p (i g r)").bitcast(FP8X4),
                 scales=scales[:].rearrange("p i g r -> p (i g r)"),

@@ -29,7 +29,8 @@ ROUNDS_BEFORE_PASSES = 2
 ROUNDS = ROW_TILES // TILES_PER_ROUND
 PSUM_BANKS = 8
 RESULT_TILES = 16
-GPSIMD_COLUMNS = 464
+GPSIMD_COLUMNS = 472
+LAST_PIECE = 256
 
 FLOPS = 2 * BATCH * PASSES * K_PASS * N_OUT
 
@@ -156,15 +157,24 @@ def tile_dynamicmemorycell_pa_t_kernel(
                     (nc.vector, slice(GPSIMD_COLUMNS, TILES_PER_ROUND * N_OUT)),
                 )
             else:
-                shares = tuple((nc.vector, slice(i * N_OUT, (i + 1) * N_OUT)) for i in range(TILES_PER_ROUND))
+                shares = tuple(
+                    (nc.vector, slice(j * LAST_PIECE, (j + 1) * LAST_PIECE))
+                    for j in range(TILES_PER_ROUND * N_OUT // LAST_PIECE)
+                )
             for engine, columns in shares:
                 engine.tensor_tensor(
                     out=flat[:, columns], in0=flat[:, columns], in1=mem_rounds[c][:, columns], op=MULT
                 )
-            count = TILES_PER_ROUND if c + 1 < ROUNDS else 1
-            for i in range(0, TILES_PER_ROUND, count):
-                first = c * TILES_PER_ROUND + i
-                nc.sync.dma_start(out=out_rows[:, first : first + count, :], in_=gate[:, i : i + count, :])
+                if c + 1 == ROUNDS:
+                    nc.sync.dma_start(
+                        out=out_rows[:, c * TILES_PER_ROUND : (c + 1) * TILES_PER_ROUND, :].rearrange(
+                            "p i n -> p (i n)"
+                        )[:, columns],
+                        in_=flat[:, columns],
+                    )
+            if c + 1 < ROUNDS:
+                first = c * TILES_PER_ROUND
+                nc.sync.dma_start(out=out_rows[:, first : first + TILES_PER_ROUND, :], in_=gate[:])
 
         quantised = {}
         gate_of = {}

from contextlib import ExitStack

import concourse.masks as masks
import concourse.mybir as mybir

F32 = mybir.dt.float32
BF16 = mybir.dt.bfloat16
I32 = mybir.dt.int32
U32 = mybir.dt.uint32
U8 = mybir.dt.uint8
FP8X4 = mybir.dt.float8_e4m3fn_x4
FP4X4 = mybir.dt.float4_e2m1fn_x4
ADD = mybir.AluOpType.add
MULT = mybir.AluOpType.mult
SIGMOID = mybir.ActivationFunctionType.Sigmoid

P = 128
PACK = 4
K_PASS = P * PACK
WORDS = K_PASS // 2
BATCH = 4096
N_OUT = 512
PASSES = 2
ROW_TILES = BATCH // P
TILES_PER_LOAD = 4
HEAD_TILES = 8
TILES_PER_ROUND = 2
ROUNDS_BEFORE_PASSES = 2
ROUNDS = ROW_TILES // TILES_PER_ROUND
PSUM_BANKS = 8
RESULT_TILES = 16
GPSIMD_COLUMNS = 472
LAST_PIECE = 256

FLOPS = 2 * BATCH * PASSES * K_PASS * N_OUT


def tile_dynamicmemorycell_pa_t_kernel(
    tc, input_tensor, previous_memory, fg_w_words, fg_w_scales, fg_b, out
):
    nc = tc.nc
    mem_rows = previous_memory.rearrange("(p r) k -> p r k", r=ROW_TILES)
    inp_rows = input_tensor.rearrange("(p r) k -> p r k", r=ROW_TILES)
    out_rows = out.rearrange("(p r) n -> p r n", r=ROW_TILES)

    head_starts = list(range(0, HEAD_TILES, TILES_PER_ROUND))
    body_starts = list(range(HEAD_TILES, ROW_TILES, TILES_PER_LOAD))

    with ExitStack() as ctx:
        consts = ctx.enter_context(tc.tile_pool(name="consts", bufs=1))
        resident = ctx.enter_context(tc.tile_pool(name="resident", bufs=2 * len(head_starts + body_starts)))
        work = ctx.enter_context(tc.tile_pool(name="work", bufs=3))
        gates = ctx.enter_context(tc.tile_pool(name="gates", bufs=RESULT_TILES // TILES_PER_ROUND))
        transposed = ctx.enter_context(tc.psum_pool(name="transposed", bufs=PSUM_BANKS // 2))
        sums = ctx.enter_context(tc.psum_pool(name="sums", bufs=PSUM_BANKS // 2))
        ctx.enter_context(tc.manual_schedule())

        bias_row = consts.tile([P, N_OUT], BF16)
        nc.vector.memset(bias_row[:], 0.0)
        ones = consts.tile([P, P], BF16)
        nc.vector.memset(ones[:], 1.0)
        bias = consts.tile([P, N_OUT], F32)

        def spread_bias():
            bias_sum = sums.tile([P, N_OUT], F32, tag="acc")
            nc.tensor.matmul(out=bias_sum[:], lhsT=ones[:], rhs=bias_row[:], start=True, stop=True)
            nc.vector.tensor_copy(out=bias[:], in_=bias_sum[:])

        w_scales = consts.tile([P, PASSES, N_OUT], U8, align_bytes=256)
        nc.vector.memset(w_scales[:].rearrange("p g n -> p (g n)").bitcast(I32), 0)
        warm = consts.tile([P, 1], F32)
        nc.vector.memset(warm[:], 0.0)
        nc.scalar.activation(out=warm[:], in_=warm[:], func=SIGMOID)
        ident = consts.tile([P, P], F32)
        masks.make_identity(nc, ident[:])

        mem_rounds = []
        inp_rounds = []

        def load_tiles(first, count):
            for rows, rounds in ((mem_rows, mem_rounds), (inp_rows, inp_rounds)):
                loaded = resident.tile([P, count, K_PASS], BF16)
                nc.sync.dma_start(out=loaded[:], in_=rows[:, first : first + count, :])
                rounds.extend(
                    [
                        loaded[:, i : i + TILES_PER_ROUND, :].rearrange("p i k -> p (i k)")
                        for i in range(0, count, TILES_PER_ROUND)
                    ]
                )

        for first in head_starts[:ROUNDS_BEFORE_PASSES]:
            load_tiles(first, TILES_PER_ROUND)
        nc.sync.dma_start(out=bias_row[0:1, :], in_=fg_b.unsqueeze(0))
        scale_rows = fg_w_scales.bitcast(I32).rearrange("g q w -> q g w")
        for quadrant in range(4):
            nc.sync.dma_start(
                out=w_scales[32 * quadrant : 32 * quadrant + 4, :, :].bitcast(I32),
                in_=scale_rows[4 * quadrant : 4 * quadrant + 4, :, :],
            )
        w_words = consts.tile([P, PASSES, 2 * N_OUT], U8, align_bytes=256)
        nc.sync.dma_start(
            out=w_words[:].bitcast(I32), in_=fg_w_words.bitcast(I32).rearrange("g p w -> p g w")
        )
        for first in head_starts[ROUNDS_BEFORE_PASSES:]:
            load_tiles(first, TILES_PER_ROUND)
        for first in body_starts:
            load_tiles(first, TILES_PER_LOAD)

        def quantise_round(c):
            grouped = work.tile([P, TILES_PER_ROUND, PASSES, P, PACK], BF16, align_bytes=256)
            for i in range(TILES_PER_ROUND):
                planes = transposed.tile([P, PASSES * 2, P], F32)
                for g, source in enumerate((mem_rounds[c], inp_rounds[c])):
                    words = source[:, i * K_PASS : (i + 1) * K_PASS].bitcast(F32)
                    for u in range(2):
                        nc.tensor.transpose(planes[:, 2 * g + u, :], words[:, u:WORDS:2], ident[:])
                nc.scalar.copy(
                    out=grouped[:, i, :, :, :]
                    .rearrange("p g r t -> p (g r t)")
                    .bitcast(F32)
                    .rearrange("p (g r u) -> p g r u", g=PASSES, u=2),
                    in_=planes[:].rearrange("p (g u) r -> p g r u", u=2),
                )
            codes = work.tile([P, TILES_PER_ROUND, PASSES, P], U32, align_bytes=256)
            scales = work.tile([P, TILES_PER_ROUND, PASSES, P], U8, align_bytes=256)
            nc.vector.quantize_mx(
                out=codes[:].rearrange("p i g r -> p (i g r)").bitcast(FP8X4),
                scales=scales[:].rearrange("p i g r -> p (i g r)"),
                in_=grouped[:].rearrange("p i g r t -> p (i g r t)"),
            )
            return codes, scales

        def multiply_round(codes, scales):
            gate = gates.tile([P, TILES_PER_ROUND, N_OUT], F32)
            for i in range(TILES_PER_ROUND):
                acc = sums.tile([P, N_OUT], F32)
                for g in range(PASSES):
                    nc.tensor.matmul_mx(
                        out=acc[:],
                        lhsT=codes[:, i, g, :].bitcast(FP8X4),
                        lhsT_scale=scales[:, i, g, :],
                        rhs=w_words[:, g, :].bitcast(FP4X4),
                        rhs_scale=w_scales[:, g, :],
                        start=(g == 0),
                        stop=(g == PASSES - 1),
                    )
                nc.vector.tensor_tensor(out=gate[:, i, :], in0=acc[:], in1=bias[:], op=ADD)
            return gate

        def finish_round(c, gate):
            for i in range(TILES_PER_ROUND):
                nc.scalar.activation(out=gate[:, i, :], in_=gate[:, i, :], func=SIGMOID)
            flat = gate[:].rearrange("p i n -> p (i n)")
            if c + 1 < ROUNDS:
                shares = (
                    (nc.gpsimd, slice(0, GPSIMD_COLUMNS)),
                    (nc.vector, slice(GPSIMD_COLUMNS, TILES_PER_ROUND * N_OUT)),
                )
            else:
                shares = tuple(
                    (nc.vector, slice(j * LAST_PIECE, (j + 1) * LAST_PIECE))
                    for j in range(TILES_PER_ROUND * N_OUT // LAST_PIECE)
                )
            for engine, columns in shares:
                engine.tensor_tensor(
                    out=flat[:, columns], in0=flat[:, columns], in1=mem_rounds[c][:, columns], op=MULT
                )
                if c + 1 == ROUNDS:
                    nc.sync.dma_start(
                        out=out_rows[:, c * TILES_PER_ROUND : (c + 1) * TILES_PER_ROUND, :].rearrange(
                            "p i n -> p (i n)"
                        )[:, columns],
                        in_=flat[:, columns],
                    )
            if c + 1 < ROUNDS:
                first = c * TILES_PER_ROUND
                nc.sync.dma_start(out=out_rows[:, first : first + TILES_PER_ROUND, :], in_=gate[:])

        quantised = {}
        gate_of = {}
        for n in range(-1, ROUNDS + 1):
            if n + 1 < ROUNDS:
                quantised[n + 1] = quantise_round(n + 1)
            if n < 0:
                spread_bias()
            elif n < ROUNDS:
                gate_of[n] = multiply_round(quantised[n][0], quantised[n][1])
            if n >= 1:
                finish_round(n - 1, gate_of[n - 1])
